import numpy as np
import ml_dtypes


def mxq(x, axis, fmt="e4m3"):
    dtype, down = {"e4m3": (ml_dtypes.float8_e4m3fn, 7), "e5m2": (ml_dtypes.float8_e5m2, 14)}[fmt]
    v = np.moveaxis(np.asarray(x, np.float32).astype(ml_dtypes.bfloat16).astype(np.float64), axis, -1)
    blocks = v.reshape(v.shape[:-1] + (-1, 32))
    amax = np.abs(blocks).max(-1, keepdims=True)
    byte = np.maximum(np.where(amax > 0, np.frexp(amax)[1] - 1 + 127, 0) - down, 1)
    scale = np.exp2(byte - 127.0)
    codes = (blocks / scale).astype(np.float32).astype(dtype).astype(np.float64)
    return np.moveaxis((codes * scale).reshape(v.shape), -1, axis)


WIDE = False


def mx_kscale(k):
    if not WIDE:
        return np.ones(k)
    levels = np.array([10, -10, 5, -5, 0])
    a = np.random.permutation(np.resize(levels, k // 512 * 4)).reshape(k // 512, 4)
    idx = np.arange(k)
    return np.exp2(a[idx // 512, idx % 128 // 32])


BF16 = ml_dtypes.bfloat16


def bf(x):
    return np.asarray(x, np.float32).astype(BF16)


def f64(x):
    return np.asarray(x).astype(np.float64)


B, S, H, U, A = 8, 1024, 1024, 128, 128
NEG = -1e20


def setup_inputs():
    s = mx_kscale(S)
    h = np.tanh(np.random.standard_normal((B, S, U)))
    h[:, :, 0] = 0.25 * h[:, :, 0] - np.log2(s)[None, :] / 16.0
    w = np.random.standard_normal((U, A)) * 5.0 / np.sqrt(U)
    w[0, :] = 16.0 * np.log(2.0)
    return {"h_tanh": bf(h),
            "W2": bf(w),
            "padding_mask": bf(np.random.random((B, S)) < 0.75),
            "data": bf(np.random.standard_normal((B, S, H)) * 5.0 * s[None, :, None] * np.mean(1.0 / s))}


def reference(h_tanh, W2, padding_mask, data):
    logits = f64(h_tanh) @ f64(W2)
    m = f64(padding_mask)[:, :, None]
    logits = logits * m + (1.0 - m) * NEG
    e = np.exp(logits - logits.max(axis=1, keepdims=True))
    attended = (mxq(e, 1, "e4m3").transpose(0, 2, 1) @ mxq(f64(data), 1, "e4m3")) / e.sum(axis=1)[:, :, None]
    return attended.mean(axis=1)

@@ -1,0 +1,260 @@
+from contextlib import ExitStack
+
+import concourse.mybir as mybir
+from concourse.masks import make_identity
+
+BF16 = mybir.dt.bfloat16
+F32 = mybir.dt.float32
+U32 = mybir.dt.uint32
+U8 = mybir.dt.uint8
+FP8X4 = mybir.dt.float8_e4m3fn_x4
+ALU = mybir.AluOpType
+ACT = mybir.ActivationFunctionType
+AXIS = mybir.AxisListType
+
+B, S, H, U, A = 8, 1024, 1024, 128, 128
+P = 128
+PACK = 4
+K_PASS = P * PACK
+PASSES = S // K_PASS
+GROUPS = PASSES * PACK
+N_TILE = 512
+N_TILES = H // N_TILE
+H_BLOCKS = H // P
+ROWS = S // P
+RUN = 4
+
+V_COLS = 640
+
+MASKED = -1e20
+OPEN = 3e38
+
+FLOPS = 2 * B * S * U * A + 2 * B * A * S * H
+
+
+def tile_selfattentionpooling_pa_t_kernel(tc, h_tanh, W2, padding_mask, data, out):
+    nc = tc.nc
+    with ExitStack() as ctx:
+        const = ctx.enter_context(tc.tile_pool(name="const", bufs=1))
+        raw_pool = ctx.enter_context(tc.tile_pool(name="raw", bufs=8))
+        grouped_pool = ctx.enter_context(tc.tile_pool(name="grouped", bufs=3))
+        codes_pool = ctx.enter_context(tc.tile_pool(name="codes", bufs=2 * PASSES))
+        work = ctx.enter_context(tc.tile_pool(name="work", bufs=2))
+        psum_t = ctx.enter_context(tc.psum_pool(name="psum_t", bufs=3))
+        psum_score = ctx.enter_context(tc.psum_pool(name="psum_score", bufs=2))
+        psum_acc = ctx.enter_context(tc.psum_pool(name="psum_acc", bufs=N_TILES))
+        psum_mean = ctx.enter_context(tc.psum_pool(name="psum_mean", bufs=1))
+        ctx.enter_context(tc.manual_schedule())
+
+        mask_rows = const.tile([P, P], BF16)
+        nc.vector.memset(mask_rows[B * ROWS : P, :], 0.0)
+        nc.scalar.dma_start(out=mask_rows[0 : B * ROWS, :], in_=padding_mask.rearrange("b (r t) -> (b r) t", t=P))
+        w2_sb = const.tile([U, A], BF16)
+        nc.scalar.dma_start(out=w2_sb[:], in_=W2[:, :])
+        h_sb = const.tile([P, B, PASSES, PACK * U], BF16)
+        h_view = h_tanh.rearrange("b (c p j) u -> p b c (j u)", c=PASSES, p=P, j=PACK)
+        nc.scalar.dma_start(out=h_sb[:, 0:1], in_=h_view[:, 0:1])
+
+        raws = {}
+        for b in range(B):
+            for c in range(PASSES):
+                raw = raw_pool.tile([P, PACK, H], BF16)
+                rows = data[b, c * K_PASS : (c + 1) * K_PASS, :]
+                nc.sync.dma_start(out=raw[:], in_=rows.rearrange("(p j) w -> p j w", j=PACK))
+                raws[(b, c)] = raw
+            if b == 0:
+                nc.sync.dma_start(out=h_sb[:, 1:B], in_=h_view[:, 1:B])
+
+        ident_bf = const.tile([P, P], BF16)
+        make_identity(nc, ident_bf[:])
+        ident_f32 = const.tile([P, P], F32)
+        make_identity(nc, ident_f32[:])
+        colsum = const.tile([A, B], F32)
+        inv_sum = const.tile([A, B], F32)
+        meanT_sb = const.tile([P, P], F32)
+        nc.vector.memset(meanT_sb[:], 0.0)
+        meanT_ps = psum_mean.tile([P, B * H_BLOCKS], F32)
+
+        maskT_ps = psum_t.tile([P, P], BF16, tag="t16")
+        nc.tensor.transpose(maskT_ps[:], mask_rows[:], ident_bf[:])
+        cap_tok = const.tile([P, B * ROWS], BF16)
+        nc.vector.tensor_scalar(
+            out=cap_tok[:],
+            in0=maskT_ps[:, 0 : B * ROWS],
+            scalar1=OPEN - MASKED,
+            scalar2=MASKED,
+            op0=ALU.mult,
+            op1=ALU.add,
+        )
+        cap_sb = const.tile([A, B, S], BF16)
+
+        cap_banks, hT_banks, score_banks, logits, eT_banks = {}, {}, {}, {}, {}
+        e_groupeds, e_words, d_words, groupeds, acc_banks = {}, {}, {}, {}, {}
+
+        def spread_caps(b):
+            cap_ps = psum_t.tile([A, ROWS, P], BF16, tag="t16")
+            for r in range(ROWS):
+                col = b * ROWS + r
+                nc.tensor.transpose(cap_ps[:, r, :], cap_tok[:, col : col + 1].to_broadcast([P, A]), ident_bf[:])
+            cap_banks[b] = cap_ps
+
+        def copy_caps(b):
+            nc.scalar.copy(out=cap_sb[:, b, :], in_=cap_banks[b][:].rearrange("a r t -> a (r t)"))
+
+        def transpose_hidden(b):
+            hT_ps = psum_t.tile([U, GROUPS, P], BF16, tag="t16")
+            for c in range(PASSES):
+                for j in range(PACK):
+                    nc.tensor.transpose(hT_ps[:, c * PACK + j, :], h_sb[:, b, c, j * U : (j + 1) * U], ident_bf[:])
+            hT_banks[b] = hT_ps
+
+        def scores(b):
+            hT_sb = work.tile([U, S], BF16)
+            nc.scalar.copy(out=hT_sb[:], in_=hT_banks[b][:].rearrange("u g p -> u (g p)"))
+            for c in range(PASSES):
+                score_ps = psum_score.tile([A, K_PASS], F32, tag="score")
+                nc.tensor.matmul(
+                    score_ps[:], lhsT=w2_sb[:], rhs=hT_sb[:, c * K_PASS : (c + 1) * K_PASS], start=True, stop=True
+                )
+                score_banks[(b, c)] = score_ps
+
+        def mask_and_max(b):
+            logit_sb = work.tile([A, S], F32)
+            for c in range(PASSES):
+                cols = slice(c * K_PASS, (c + 1) * K_PASS)
+                nc.vector.tensor_tensor(
+                    out=logit_sb[:, cols].rearrange("a (j p) -> a j p", j=PACK),
+                    in0=score_banks[(b, c)][:].rearrange("a (j p) -> a j p", j=PACK),
+                    in1=cap_sb[:, b, cols].rearrange("a (p j) -> a j p", j=PACK),
+                    op=ALU.min,
+                )
+            neg_max = work.tile([A, 1], F32)
+            nc.vector.tensor_reduce(out=neg_max[:], in_=logit_sb[:], axis=AXIS.X, op=ALU.max, negate=True)
+            logits[b] = (logit_sb, neg_max)
+
+        def exponentials(b):
+            logit_sb, neg_max = logits[b]
+            e_sb = work.tile([A, S], BF16)
+            nc.scalar.activation(
+                out=e_sb[:], in_=logit_sb[:], func=ACT.Exp, bias=neg_max[:], scale=1.0, accum_out=colsum[:, b : b + 1]
+            )
+            eT_ps = psum_t.tile([P, GROUPS, A], BF16, tag="t16")
+            for g in range(GROUPS):
+                nc.tensor.transpose(eT_ps[:, g, :], e_sb[:, g * P : (g + 1) * P], ident_bf[:])
+            eT_banks[b] = eT_ps
+
+        def regroup_e(b):
+            e_grouped = work.tile([P, PASSES, A, PACK], BF16, align_bytes=64)
+            nc.scalar.copy(out=e_grouped[:], in_=eT_banks[b][:].rearrange("p (c j) a -> p c a j", j=PACK))
+            e_groupeds[b] = e_grouped
+
+        def quantise_e(b):
+            e_codes = work.tile([P, PASSES * A], U32, align_bytes=64)
+            e_scales = work.tile([P, PASSES * A], U8, align_bytes=64)
+            nc.vector.quantize_mx(
+                out=e_codes[:].bitcast(FP8X4),
+                scales=e_scales[:],
+                in_=e_groupeds[b][:].rearrange("p c a j -> p (c a j)"),
+            )
+            e_words[b] = (e_codes, e_scales)
+
+        def regroup_data(b, c):
+            raw = raws[(b, c)]
+            grouped = grouped_pool.tile([P, H, PACK], BF16, align_bytes=64)
+            v_cols = slice(0, V_COLS)
+            s_cols = slice(V_COLS, H)
+            nc.vector.tensor_copy(
+                out=grouped[:, v_cols, :].rearrange("p (q i) j -> p q j i", i=RUN),
+                in_=raw[:, :, v_cols].rearrange("p j (q i) -> p q j i", i=RUN),
+            )
+            nc.scalar.copy(
+                out=grouped[:, s_cols, :].rearrange("p (q i) j -> p q j i", i=RUN),
+                in_=raw[:, :, s_cols].rearrange("p j (q i) -> p q j i", i=RUN),
+            )
+            groupeds[(b, c)] = grouped
+
+        def quantise_data(b, c):
+            d_codes = codes_pool.tile([P, H], U32, align_bytes=64)
+            d_scales = codes_pool.tile([P, H], U8, align_bytes=64)
+            nc.vector.quantize_mx(
+                out=d_codes[:].bitcast(FP8X4),
+                scales=d_scales[:],
+                in_=groupeds[(b, c)][:].rearrange("p w j -> p (w j)"),
+            )
+            d_words[(b, c)] = (d_codes, d_scales)
+
+        def attend(b):
+            e_codes, e_scales = e_words[b]
+            banks = []
+            for n in range(N_TILES):
+                acc_ps = psum_acc.tile([A, N_TILE], F32, tag="acc")
+                n_cols = slice(n * N_TILE, (n + 1) * N_TILE)
+                for c in range(PASSES):
+                    d_codes, d_scales = d_words[(b, c)]
+                    a_cols = slice(c * A, (c + 1) * A)
+                    nc.tensor.matmul_mx(
+                        out=acc_ps[:],
+                        lhsT=e_codes[:, a_cols].bitcast(FP8X4),
+                        lhsT_scale=e_scales[:, a_cols],
+                        rhs=d_codes[:, n_cols].bitcast(FP8X4),
+                        rhs_scale=d_scales[:, n_cols],
+                        start=(c == 0),
+                        stop=(c == PASSES - 1),
+                    )
+                banks.append(acc_ps)
+            acc_banks[b] = banks
+
+        def mean_over_heads(b):
+            acc_sb = work.tile([A, H], F32)
+            for n in range(N_TILES):
+                nc.scalar.copy(out=acc_sb[:, n * N_TILE : (n + 1) * N_TILE], in_=acc_banks[b][n][:])
+            nc.vector.reciprocal(out=inv_sum[:, b : b + 1], in_=colsum[:, b : b + 1])
+            for q in range(H_BLOCKS):
+                col = b * H_BLOCKS + q
+                nc.tensor.matmul(
+                    meanT_ps[:, col : col + 1],
+                    lhsT=acc_sb[:, q * P : (q + 1) * P],
+                    rhs=inv_sum[:, b : b + 1],
+                    start=True,
+                    stop=True,
+                )
+
+        transpose_hidden(0)
+        spread_caps(0)
+        scores(0)
+        copy_caps(0)
+        for b in range(B + 1):
+            has_this = b < B
+            has_last = b >= 1
+            has_next = b + 1 < B
+            if has_this:
+                regroup_data(b, 0)
+            if has_last:
+                quantise_e(b - 1)
+                attend(b - 1)
+            if has_this:
+                mask_and_max(b)
+            if has_next:
+                transpose_hidden(b + 1)
+                spread_caps(b + 1)
+            if has_this:
+                quantise_data(b, 0)
+                regroup_data(b, 1)
+            if has_next:
+                copy_caps(b + 1)
+            if has_this:
+                exponentials(b)
+            if has_last:
+                mean_over_heads(b - 1)
+            if has_this:
+                regroup_e(b)
+                quantise_data(b, 1)
+            if has_next:
+                scores(b + 1)
+
+        nc.scalar.mul(out=meanT_sb[:, 0 : B * H_BLOCKS], in_=meanT_ps[:], mul=1.0 / A)
+        mean_ps = psum_score.tile([P, P], F32, tag="score")
+        nc.tensor.transpose(mean_ps[:], meanT_sb[:], ident_f32[:])
+        mean_sb = const.tile([P, P], F32)
+        nc.scalar.copy(out=mean_sb[:], in_=mean_ps[:])
+        nc.sync.dma_start(out=out.rearrange("b (q h) -> (b q) h", h=P), in_=mean_sb[0 : B * H_BLOCKS, :])

@@ -21,13 +21,11 @@ GROUPS = PASSES * PACK
 N_TILE = 512
 N_TILES = H // N_TILE
 H_BLOCKS = H // P
-ROWS = S // P
 RUN = 4
 
-V_COLS = 640
+V_COLS = 768
 
 MASKED = -1e20
-OPEN = 3e38
 
 FLOPS = 2 * B * S * U * A + 2 * B * A * S * H
 
@@ -46,14 +44,16 @@ def tile_selfattentionpooling_pa_t_kernel(tc, h_tanh, W2, padding_mask, data, ou
         psum_mean = ctx.enter_context(tc.psum_pool(name="psum_mean", bufs=1))
         ctx.enter_context(tc.manual_schedule())
 
-        mask_rows = const.tile([P, P], BF16)
-        nc.vector.memset(mask_rows[B * ROWS : P, :], 0.0)
-        nc.scalar.dma_start(out=mask_rows[0 : B * ROWS, :], in_=padding_mask.rearrange("b (r t) -> (b r) t", t=P))
+        mask_rows = const.tile([P, K_PASS], BF16)
+        nc.vector.memset(mask_rows[:], 0.0)
         w2_sb = const.tile([U, A], BF16)
-        nc.scalar.dma_start(out=w2_sb[:], in_=W2[:, :])
+        nc.sync.dma_start(out=w2_sb[:], in_=W2[:, :])
         h_sb = const.tile([P, B, PASSES, PACK * U], BF16)
         h_view = h_tanh.rearrange("b (c p j) u -> p b c (j u)", c=PASSES, p=P, j=PACK)
-        nc.scalar.dma_start(out=h_sb[:, 0:1], in_=h_view[:, 0:1])
+        nc.sync.dma_start(out=h_sb[:, 0:1], in_=h_view[:, 0:1])
+        nc.sync.dma_start(
+            out=mask_rows[0 : B * PASSES, :], in_=padding_mask.rearrange("b (c k) -> (b c) k", k=K_PASS)
+        )
 
         raws = {}
         for b in range(B):
@@ -69,37 +69,30 @@ def tile_selfattentionpooling_pa_t_kernel(tc, h_tanh, W2, padding_mask, data, ou
         make_identity(nc, ident_bf[:])
         ident_f32 = const.tile([P, P], F32)
         make_identity(nc, ident_f32[:])
+        bank_sum = const.tile([A, B, PASSES], F32)
         colsum = const.tile([A, B], F32)
         inv_sum = const.tile([A, B], F32)
         meanT_sb = const.tile([P, P], F32)
         nc.vector.memset(meanT_sb[:], 0.0)
         meanT_ps = psum_mean.tile([P, B * H_BLOCKS], F32)
 
-        maskT_ps = psum_t.tile([P, P], BF16, tag="t16")
-        nc.tensor.transpose(maskT_ps[:], mask_rows[:], ident_bf[:])
-        cap_tok = const.tile([P, B * ROWS], BF16)
+        maskT_ps = psum_t.tile([P, PACK, P], BF16, tag="t16")
+        for j in range(PACK):
+            nc.tensor.transpose(
+                maskT_ps[:, j, :], mask_rows[:].rearrange("r (p j) -> r j p", j=PACK)[:, j, :], ident_bf[:]
+            )
+        penalty = const.tile([P, PACK, B * PASSES], F32)
         nc.vector.tensor_scalar(
-            out=cap_tok[:],
-            in0=maskT_ps[:, 0 : B * ROWS],
-            scalar1=OPEN - MASKED,
-            scalar2=MASKED,
-            op0=ALU.mult,
-            op1=ALU.add,
+            out=penalty[:],
+            in0=maskT_ps[:, :, 0 : B * PASSES],
+            scalar1=1.0,
+            scalar2=-MASKED,
+            op0=ALU.subtract,
+            op1=ALU.mult,
         )
-        cap_sb = const.tile([A, B, S], BF16)
 
-        cap_banks, hT_banks, score_banks, logits, eT_banks = {}, {}, {}, {}, {}
+        hT_banks, score_banks, neg_maxes, eT_banks = {}, {}, {}, {}
         e_groupeds, e_words, d_words, groupeds, acc_banks = {}, {}, {}, {}, {}
-
-        def spread_caps(b):
-            cap_ps = psum_t.tile([A, ROWS, P], BF16, tag="t16")
-            for r in range(ROWS):
-                col = b * ROWS + r
-                nc.tensor.transpose(cap_ps[:, r, :], cap_tok[:, col : col + 1].to_broadcast([P, A]), ident_bf[:])
-            cap_banks[b] = cap_ps
-
-        def copy_caps(b):
-            nc.scalar.copy(out=cap_sb[:, b, :], in_=cap_banks[b][:].rearrange("a r t -> a (r t)"))
 
         def transpose_hidden(b):
             hT_ps = psum_t.tile([U, GROUPS, P], BF16, tag="t16")
@@ -112,32 +105,41 @@ def tile_selfattentionpooling_pa_t_kernel(tc, h_tanh, W2, padding_mask, data, ou
             hT_sb = work.tile([U, S], BF16)
             nc.scalar.copy(out=hT_sb[:], in_=hT_banks[b][:].rearrange("u g p -> u (g p)"))
             for c in range(PASSES):
-                score_ps = psum_score.tile([A, K_PASS], F32, tag="score")
+                logit_ps = psum_score.tile([A, K_PASS], F32, tag="score")
                 nc.tensor.matmul(
-                    score_ps[:], lhsT=w2_sb[:], rhs=hT_sb[:, c * K_PASS : (c + 1) * K_PASS], start=True, stop=True
+                    logit_ps[:], lhsT=w2_sb[:], rhs=hT_sb[:, c * K_PASS : (c + 1) * K_PASS], start=True, stop=False
                 )
-                score_banks[(b, c)] = score_ps
+                row = b * PASSES + c
+                for j in range(PACK):
+                    nc.tensor.matmul(
+                        logit_ps[:, j * P : (j + 1) * P],
+                        lhsT=penalty[:, j, row : row + 1].to_broadcast([P, A]),
+                        rhs=ident_f32[:],
+                        is_transpose=True,
+                        start=False,
+                        stop=(j == PACK - 1),
+                    )
+                score_banks[(b, c)] = logit_ps
 
-        def mask_and_max(b):
-            logit_sb = work.tile([A, S], F32)
+        def maxima(b):
+            bank_max = work.tile([A, PASSES], F32)
             for c in range(PASSES):
-                cols = slice(c * K_PASS, (c + 1) * K_PASS)
-                nc.vector.tensor_tensor(
-                    out=logit_sb[:, cols].rearrange("a (j p) -> a j p", j=PACK),
-                    in0=score_banks[(b, c)][:].rearrange("a (j p) -> a j p", j=PACK),
-                    in1=cap_sb[:, b, cols].rearrange("a (p j) -> a j p", j=PACK),
-                    op=ALU.min,
-                )
+                nc.vector.tensor_reduce(out=bank_max[:, c : c + 1], in_=score_banks[(b, c)][:], axis=AXIS.X, op=ALU.max)
             neg_max = work.tile([A, 1], F32)
-            nc.vector.tensor_reduce(out=neg_max[:], in_=logit_sb[:], axis=AXIS.X, op=ALU.max, negate=True)
-            logits[b] = (logit_sb, neg_max)
+            nc.vector.tensor_reduce(out=neg_max[:], in_=bank_max[:], axis=AXIS.X, op=ALU.max, negate=True)
+            neg_maxes[b] = neg_max
 
         def exponentials(b):
-            logit_sb, neg_max = logits[b]
             e_sb = work.tile([A, S], BF16)
-            nc.scalar.activation(
-                out=e_sb[:], in_=logit_sb[:], func=ACT.Exp, bias=neg_max[:], scale=1.0, accum_out=colsum[:, b : b + 1]
-            )
+            for c in range(PASSES):
+                nc.scalar.activation(
+                    out=e_sb[:, c * K_PASS : (c + 1) * K_PASS],
+                    in_=score_banks[(b, c)][:],
+                    func=ACT.Exp,
+                    bias=neg_maxes[b][:],
+                    scale=1.0,
+                    accum_out=bank_sum[:, b, c : c + 1],
+                )
             eT_ps = psum_t.tile([P, GROUPS, A], BF16, tag="t16")
             for g in range(GROUPS):
                 nc.tensor.transpose(eT_ps[:, g, :], e_sb[:, g * P : (g + 1) * P], ident_bf[:])
@@ -204,11 +206,14 @@ def tile_selfattentionpooling_pa_t_kernel(tc, h_tanh, W2, padding_mask, data, ou
                 banks.append(acc_ps)
             acc_banks[b] = banks
 
+        def reciprocal_sums(b):
+            nc.vector.tensor_reduce(out=colsum[:, b : b + 1], in_=bank_sum[:, b, :], axis=AXIS.X, op=ALU.add)
+            nc.vector.reciprocal(out=inv_sum[:, b : b + 1], in_=colsum[:, b : b + 1])
+
         def mean_over_heads(b):
             acc_sb = work.tile([A, H], F32)
             for n in range(N_TILES):
                 nc.scalar.copy(out=acc_sb[:, n * N_TILE : (n + 1) * N_TILE], in_=acc_banks[b][n][:])
-            nc.vector.reciprocal(out=inv_sum[:, b : b + 1], in_=colsum[:, b : b + 1])
             for q in range(H_BLOCKS):
                 col = b * H_BLOCKS + q
                 nc.tensor.matmul(
@@ -220,9 +225,7 @@ def tile_selfattentionpooling_pa_t_kernel(tc, h_tanh, W2, padding_mask, data, ou
                 )
 
         transpose_hidden(0)
-        spread_caps(0)
         scores(0)
-        copy_caps(0)
         for b in range(B + 1):
             has_this = b < B
             has_last = b >= 1
@@ -231,26 +234,24 @@ def tile_selfattentionpooling_pa_t_kernel(tc, h_tanh, W2, padding_mask, data, ou
                 regroup_data(b, 0)
             if has_last:
                 quantise_e(b - 1)
+                reciprocal_sums(b - 1)
                 attend(b - 1)
             if has_this:
-                mask_and_max(b)
+                maxima(b)
             if has_next:
                 transpose_hidden(b + 1)
-                spread_caps(b + 1)
             if has_this:
                 quantise_data(b, 0)
                 regroup_data(b, 1)
-            if has_next:
-                copy_caps(b + 1)
-            if has_this:
-                exponentials(b)
             if has_last:
                 mean_over_heads(b - 1)
             if has_this:
-                regroup_e(b)
-                quantise_data(b, 1)
+                exponentials(b)
             if has_next:
                 scores(b + 1)
+            if has_this:
+                regroup_e(b)
+                quantise_data(b, 1)
 
         nc.scalar.mul(out=meanT_sb[:, 0 : B * H_BLOCKS], in_=meanT_ps[:], mul=1.0 / A)
         mean_ps = psum_score.tile([P, P], F32, tag="score")

@@ -91,8 +91,8 @@ def tile_selfattentionpooling_pa_t_kernel(tc, h_tanh, W2, padding_mask, data, ou
             op1=ALU.mult,
         )
 
-        hT_banks, score_banks, neg_maxes, eT_banks = {}, {}, {}, {}
-        e_groupeds, e_words, d_words, groupeds, acc_banks = {}, {}, {}, {}, {}
+        hT_banks, score_banks, bank_maxes, neg_maxes, eT_banks = {}, {}, {}, {}, {}
+        e_groupeds, e_words, d_words, groupeds, acc_banks, attendeds = {}, {}, {}, {}, {}, {}
 
         def transpose_hidden(b):
             hT_ps = psum_t.tile([U, GROUPS, P], BF16, tag="t16")
@@ -121,12 +121,15 @@ def tile_selfattentionpooling_pa_t_kernel(tc, h_tanh, W2, padding_mask, data, ou
                     )
                 score_banks[(b, c)] = logit_ps
 
-        def maxima(b):
+        def bank_maxima(b):
             bank_max = work.tile([A, PASSES], F32)
             for c in range(PASSES):
                 nc.vector.tensor_reduce(out=bank_max[:, c : c + 1], in_=score_banks[(b, c)][:], axis=AXIS.X, op=ALU.max)
+            bank_maxes[b] = bank_max
+
+        def negative_maximum(b):
             neg_max = work.tile([A, 1], F32)
-            nc.vector.tensor_reduce(out=neg_max[:], in_=bank_max[:], axis=AXIS.X, op=ALU.max, negate=True)
+            nc.vector.tensor_reduce(out=neg_max[:], in_=bank_maxes[b][:], axis=AXIS.X, op=ALU.max, negate=True)
             neg_maxes[b] = neg_max
 
         def exponentials(b):
@@ -206,19 +209,24 @@ def tile_selfattentionpooling_pa_t_kernel(tc, h_tanh, W2, padding_mask, data, ou
                 banks.append(acc_ps)
             acc_banks[b] = banks
 
-        def reciprocal_sums(b):
+        def sum_e(b):
             nc.vector.tensor_reduce(out=colsum[:, b : b + 1], in_=bank_sum[:, b, :], axis=AXIS.X, op=ALU.add)
+
+        def reciprocal_sum(b):
             nc.vector.reciprocal(out=inv_sum[:, b : b + 1], in_=colsum[:, b : b + 1])
 
-        def mean_over_heads(b):
+        def copy_attended(b):
             acc_sb = work.tile([A, H], F32)
             for n in range(N_TILES):
                 nc.scalar.copy(out=acc_sb[:, n * N_TILE : (n + 1) * N_TILE], in_=acc_banks[b][n][:])
+            attendeds[b] = acc_sb
+
+        def mean_over_heads(b):
             for q in range(H_BLOCKS):
                 col = b * H_BLOCKS + q
                 nc.tensor.matmul(
                     meanT_ps[:, col : col + 1],
-                    lhsT=acc_sb[:, q * P : (q + 1) * P],
+                    lhsT=attendeds[b][:, q * P : (q + 1) * P],
                     rhs=inv_sum[:, b : b + 1],
                     start=True,
                     stop=True,
@@ -232,24 +240,30 @@ def tile_selfattentionpooling_pa_t_kernel(tc, h_tanh, W2, padding_mask, data, ou
             has_next = b + 1 < B
             if has_this:
                 regroup_data(b, 0)
+                bank_maxima(b)
             if has_last:
                 quantise_e(b - 1)
-                reciprocal_sums(b - 1)
-                attend(b - 1)
             if has_this:
-                maxima(b)
+                negative_maximum(b)
+            if has_last:
+                sum_e(b - 1)
+                attend(b - 1)
             if has_next:
                 transpose_hidden(b + 1)
             if has_this:
-                quantise_data(b, 0)
                 regroup_data(b, 1)
+            if has_last:
+                reciprocal_sum(b - 1)
+            if has_this:
+                exponentials(b)
+            if has_last:
+                copy_attended(b - 1)
+            if has_next:
+                scores(b + 1)
             if has_last:
                 mean_over_heads(b - 1)
             if has_this:
-                exponentials(b)
-            if has_next:
-                scores(b + 1)
-            if has_this:
+                quantise_data(b, 0)
                 regroup_e(b)
                 quantise_data(b, 1)
 

@@ -23,7 +23,8 @@ N_TILES = H // N_TILE
 H_BLOCKS = H // P
 RUN = 4
 
-V_COLS = 768
+V_COLS = 672
+S_COLS = 256
 
 MASKED = -1e20
 
@@ -167,7 +168,8 @@ def tile_selfattentionpooling_pa_t_kernel(tc, h_tanh, W2, padding_mask, data, ou
             raw = raws[(b, c)]
             grouped = grouped_pool.tile([P, H, PACK], BF16, align_bytes=64)
             v_cols = slice(0, V_COLS)
-            s_cols = slice(V_COLS, H)
+            s_cols = slice(V_COLS, V_COLS + S_COLS)
+            g_cols = slice(V_COLS + S_COLS, H)
             nc.vector.tensor_copy(
                 out=grouped[:, v_cols, :].rearrange("p (q i) j -> p q j i", i=RUN),
                 in_=raw[:, :, v_cols].rearrange("p j (q i) -> p q j i", i=RUN),
@@ -175,6 +177,14 @@ def tile_selfattentionpooling_pa_t_kernel(tc, h_tanh, W2, padding_mask, data, ou
             nc.scalar.copy(
                 out=grouped[:, s_cols, :].rearrange("p (q i) j -> p q j i", i=RUN),
                 in_=raw[:, :, s_cols].rearrange("p j (q i) -> p q j i", i=RUN),
+            )
+            nc.gpsimd.tensor_scalar(
+                out=grouped[:, g_cols, :].rearrange("p (q i) j -> p q j i", i=RUN),
+                in0=raw[:, :, g_cols].rearrange("p j (q i) -> p q j i", i=RUN),
+                scalar1=1.0,
+                scalar2=0.0,
+                op0=ALU.mult,
+                op1=ALU.add,
             )
             groupeds[(b, c)] = grouped
 

@@ -21,10 +21,11 @@ GROUPS = PASSES * PACK
 N_TILE = 512
 N_TILES = H // N_TILE
 H_BLOCKS = H // P
+PAIRS = PACK // 2
 RUN = 4
 
-V_COLS = 672
-S_COLS = 256
+V_COLS = 576
+S_COLS = 352
 
 MASKED = -1e20
 
@@ -60,11 +61,15 @@ def tile_selfattentionpooling_pa_t_kernel(tc, h_tanh, W2, padding_mask, data, ou
         for b in range(B):
             for c in range(PASSES):
                 raw = raw_pool.tile([P, PACK, H], BF16)
-                rows = data[b, c * K_PASS : (c + 1) * K_PASS, :]
-                nc.sync.dma_start(out=raw[:], in_=rows.rearrange("(p j) w -> p j w", j=PACK))
+                rows = data[b, c * K_PASS : (c + 1) * K_PASS, :].rearrange("(p j) w -> p j w", j=PACK)
+                if b == 0 and c == 0:
+                    nc.sync.dma_start(out=raw[:, :, 0:V_COLS], in_=rows[:, :, 0:V_COLS])
+                    nc.sync.dma_start(out=raw[:, :, V_COLS:H], in_=rows[:, :, V_COLS:H])
+                else:
+                    nc.sync.dma_start(out=raw[:], in_=rows)
                 raws[(b, c)] = raw
-            if b == 0:
-                nc.sync.dma_start(out=h_sb[:, 1:B], in_=h_view[:, 1:B])
+                if c == 0 and b + 1 < B:
+                    nc.sync.dma_start(out=h_sb[:, b + 1 : b + 2], in_=h_view[:, b + 1 : b + 2])
 
         ident_bf = const.tile([P, P], BF16)
         make_identity(nc, ident_bf[:])
@@ -137,21 +142,30 @@ def tile_selfattentionpooling_pa_t_kernel(tc, h_tanh, W2, padding_mask, data, ou
             e_sb = work.tile([A, S], BF16)
             for c in range(PASSES):
                 nc.scalar.activation(
-                    out=e_sb[:, c * K_PASS : (c + 1) * K_PASS],
-                    in_=score_banks[(b, c)][:],
+                    out=e_sb[:, c * K_PASS : (c + 1) * K_PASS].rearrange("a (p j) -> a p j", j=PACK),
+                    in_=score_banks[(b, c)][:].rearrange("a (j p) -> a p j", j=PACK),
                     func=ACT.Exp,
                     bias=neg_maxes[b][:],
                     scale=1.0,
                     accum_out=bank_sum[:, b, c : c + 1],
                 )
-            eT_ps = psum_t.tile([P, GROUPS, A], BF16, tag="t16")
-            for g in range(GROUPS):
-                nc.tensor.transpose(eT_ps[:, g, :], e_sb[:, g * P : (g + 1) * P], ident_bf[:])
+            e_pairs = e_sb[:].bitcast(F32)
+            eT_ps = psum_t.tile([P, PASSES, PAIRS, A], F32, tag="t16")
+            for c in range(PASSES):
+                for u in range(PAIRS):
+                    nc.tensor.transpose(
+                        eT_ps[:, c, u, :],
+                        e_pairs[:, c * PAIRS * P + u : (c + 1) * PAIRS * P : PAIRS],
+                        ident_f32[:],
+                    )
             eT_banks[b] = eT_ps
 
         def regroup_e(b):
-            e_grouped = work.tile([P, PASSES, A, PACK], BF16, align_bytes=64)
-            nc.scalar.copy(out=e_grouped[:], in_=eT_banks[b][:].rearrange("p (c j) a -> p c a j", j=PACK))
+            e_grouped = work.tile([P, PASSES * A * PACK], BF16, align_bytes=64)
+            nc.scalar.copy(
+                out=e_grouped[:].bitcast(F32).rearrange("p (c a u) -> p c a u", c=PASSES, u=PAIRS),
+                in_=eT_banks[b][:].rearrange("p c u a -> p c a u"),
+            )
             e_groupeds[b] = e_grouped
 
         def quantise_e(b):
@@ -160,7 +174,7 @@ def tile_selfattentionpooling_pa_t_kernel(tc, h_tanh, W2, padding_mask, data, ou
             nc.vector.quantize_mx(
                 out=e_codes[:].bitcast(FP8X4),
                 scales=e_scales[:],
-                in_=e_groupeds[b][:].rearrange("p c a j -> p (c a j)"),
+                in_=e_groupeds[b][:],
             )
             e_words[b] = (e_codes, e_scales)
 

@@ -24,8 +24,8 @@ H_BLOCKS = H // P
 PAIRS = PACK // 2
 RUN = 4
 
-V_COLS = 576
-S_COLS = 352
+V_COLS = 592
+S_COLS = 336
 
 MASKED = -1e20
 

@@ -29,6 +29,10 @@ S_COLS = 336
 
 MASKED = -1e20
 
+COLUMN_SEQS = (0, 1, 2)
+ROW_SEQS = (3, 4, 5, 6)
+LAST = 7
+
 FLOPS = 2 * B * S * U * A + 2 * B * A * S * H
 
 
@@ -40,10 +44,10 @@ def tile_selfattentionpooling_pa_t_kernel(tc, h_tanh, W2, padding_mask, data, ou
         grouped_pool = ctx.enter_context(tc.tile_pool(name="grouped", bufs=3))
         codes_pool = ctx.enter_context(tc.tile_pool(name="codes", bufs=2 * PASSES))
         work = ctx.enter_context(tc.tile_pool(name="work", bufs=2))
-        psum_t = ctx.enter_context(tc.psum_pool(name="psum_t", bufs=3))
+        psum_t = ctx.enter_context(tc.psum_pool(name="psum_t", bufs=2))
         psum_score = ctx.enter_context(tc.psum_pool(name="psum_score", bufs=2))
         psum_acc = ctx.enter_context(tc.psum_pool(name="psum_acc", bufs=N_TILES))
-        psum_mean = ctx.enter_context(tc.psum_pool(name="psum_mean", bufs=1))
+        psum_mean = ctx.enter_context(tc.psum_pool(name="psum_mean", bufs=2))
         ctx.enter_context(tc.manual_schedule())
 
         mask_rows = const.tile([P, K_PASS], BF16)
@@ -80,7 +84,12 @@ def tile_selfattentionpooling_pa_t_kernel(tc, h_tanh, W2, padding_mask, data, ou
         inv_sum = const.tile([A, B], F32)
         meanT_sb = const.tile([P, P], F32)
         nc.vector.memset(meanT_sb[:], 0.0)
-        meanT_ps = psum_mean.tile([P, B * H_BLOCKS], F32)
+        meanT_ps = psum_mean.tile([P, len(COLUMN_SEQS) * H_BLOCKS], F32, tag="mean")
+        one_hot = const.tile([A, len(ROW_SEQS), P], F32)
+        nc.gpsimd.memset(one_hot[:], 0.0)
+        inv_row = const.tile([P, A], F32)
+        rows_sb = const.tile([P, H], F32)
+        row_banks = []
 
         maskT_ps = psum_t.tile([P, PACK, P], BF16, tag="t16")
         for j in range(PACK):
@@ -237,13 +246,17 @@ def tile_selfattentionpooling_pa_t_kernel(tc, h_tanh, W2, padding_mask, data, ou
             nc.vector.tensor_reduce(out=colsum[:, b : b + 1], in_=bank_sum[:, b, :], axis=AXIS.X, op=ALU.add)
 
         def reciprocal_sum(b):
-            nc.vector.reciprocal(out=inv_sum[:, b : b + 1], in_=colsum[:, b : b + 1])
+            if b in ROW_SEQS:
+                r = ROW_SEQS.index(b)
+                nc.vector.reciprocal(out=one_hot[:, r, r : r + 1], in_=colsum[:, b : b + 1])
+            else:
+                nc.vector.reciprocal(out=inv_sum[:, b : b + 1], in_=colsum[:, b : b + 1])
 
-        def copy_attended(b):
-            acc_sb = work.tile([A, H], F32)
-            for n in range(N_TILES):
-                nc.scalar.copy(out=acc_sb[:, n * N_TILE : (n + 1) * N_TILE], in_=acc_banks[b][n][:])
-            attendeds[b] = acc_sb
+        def copy_attended(b, n):
+            if n == 0:
+                acc_sb = work.tile([A, H], F32)
+                attendeds[b] = acc_sb
+            nc.scalar.copy(out=attendeds[b][:, n * N_TILE : (n + 1) * N_TILE], in_=acc_banks[b][n][:])
 
         def mean_over_heads(b):
             for q in range(H_BLOCKS):
@@ -256,44 +269,120 @@ def tile_selfattentionpooling_pa_t_kernel(tc, h_tanh, W2, padding_mask, data, ou
                     stop=True,
                 )
 
+        def mean_as_row(b):
+            r = ROW_SEQS.index(b)
+            for n in range(N_TILES):
+                if r == 0:
+                    row_ps = psum_mean.tile([P, N_TILE], F32, tag="mean")
+                    row_banks.append(row_ps)
+                nc.tensor.matmul(
+                    row_banks[n][:],
+                    lhsT=one_hot[:, r, :],
+                    rhs=attendeds[b][:, n * N_TILE : (n + 1) * N_TILE],
+                    start=(r == 0),
+                    stop=(r == len(ROW_SEQS) - 1),
+                )
+
+        def copy_columns():
+            cols = len(COLUMN_SEQS) * H_BLOCKS
+            nc.scalar.mul(out=meanT_sb[:, 0:cols], in_=meanT_ps[:], mul=1.0 / A)
+
+        def store_rows():
+            rows = len(ROW_SEQS)
+            for n in range(N_TILES):
+                nc.scalar.mul(out=rows_sb[0:rows, n * N_TILE : (n + 1) * N_TILE], in_=row_banks[n][0:rows, :], mul=1.0 / A)
+            nc.sync.dma_start(out=out[ROW_SEQS[0] : ROW_SEQS[0] + rows, :], in_=rows_sb[0:rows, :])
+
+        def broadcast_reciprocals(b):
+            bc_ps = psum_t.tile([P, A], F32, tag="t16")
+            nc.tensor.transpose(bc_ps[:], inv_sum[:, b : b + 1].to_broadcast([A, P]), ident_f32[:])
+            nc.scalar.mul(out=inv_row[:], in_=bc_ps[:], mul=1.0 / A)
+
+        def attend_by_features(b):
+            e_codes, e_scales = e_words[b]
+            spare = [(psum_score, "score"), (psum_score, "score"), (psum_acc, "acc"), (psum_acc, "acc"), (psum_t, "t16"), (psum_t, "t16")]
+            for q in range(H_BLOCKS):
+                pool, tag = spare[q % len(spare)]
+                accT_ps = pool.tile([P, A], F32, tag=tag)
+                w_cols = slice(q * P, (q + 1) * P)
+                for c in range(PASSES):
+                    d_codes, d_scales = d_words[(b, c)]
+                    a_cols = slice(c * A, (c + 1) * A)
+                    nc.tensor.matmul_mx(
+                        out=accT_ps[:],
+                        lhsT=d_codes[:, w_cols].bitcast(FP8X4),
+                        lhsT_scale=d_scales[:, w_cols],
+                        rhs=e_codes[:, a_cols].bitcast(FP8X4),
+                        rhs_scale=e_scales[:, a_cols],
+                        start=(c == 0),
+                        stop=(c == PASSES - 1),
+                    )
+                weighted = work.tile([P, A], F32)
+                col = len(COLUMN_SEQS) * H_BLOCKS + q
+                nc.vector.scalar_tensor_tensor(
+                    out=weighted[:],
+                    in0=accT_ps[:],
+                    scalar=1.0,
+                    in1=inv_row[:],
+                    op0=ALU.mult,
+                    op1=ALU.mult,
+                    accum_out=meanT_sb[:, col : col + 1],
+                )
+
         transpose_hidden(0)
         scores(0)
-        for b in range(B + 1):
-            has_this = b < B
+        for b in range(B):
             has_last = b >= 1
             has_next = b + 1 < B
-            if has_this:
-                regroup_data(b, 0)
-                bank_maxima(b)
+            regroup_data(b, 0)
+            bank_maxima(b)
             if has_last:
                 quantise_e(b - 1)
-            if has_this:
-                negative_maximum(b)
+            negative_maximum(b)
             if has_last:
                 sum_e(b - 1)
                 attend(b - 1)
             if has_next:
                 transpose_hidden(b + 1)
-            if has_this:
-                regroup_data(b, 1)
+            regroup_data(b, 1)
             if has_last:
                 reciprocal_sum(b - 1)
-            if has_this:
-                exponentials(b)
+            exponentials(b)
             if has_last:
-                copy_attended(b - 1)
+                copy_attended(b - 1, 0)
+            if not has_next:
+                regroup_e(b)
+            if has_last:
+                copy_attended(b - 1, 1)
+            if b - 1 == ROW_SEQS[0]:
+                copy_columns()
             if has_next:
                 scores(b + 1)
-            if has_last:
+            if b - 1 in COLUMN_SEQS:
                 mean_over_heads(b - 1)
-            if has_this:
-                quantise_data(b, 0)
+            if b - 1 in ROW_SEQS:
+                mean_as_row(b - 1)
+            quantise_data(b, 0)
+            if has_next:
                 regroup_e(b)
-                quantise_data(b, 1)
+            else:
+                sum_e(b)
+                quantise_e(b)
+                reciprocal_sum(b)
+                broadcast_reciprocals(b)
+            quantise_data(b, 1)
 
-        nc.scalar.mul(out=meanT_sb[:, 0 : B * H_BLOCKS], in_=meanT_ps[:], mul=1.0 / A)
+        attend_by_features(LAST)
+        store_rows()
+
         mean_ps = psum_score.tile([P, P], F32, tag="score")
         nc.tensor.transpose(mean_ps[:], meanT_sb[:], ident_f32[:])
         mean_sb = const.tile([P, P], F32)
         nc.scalar.copy(out=mean_sb[:], in_=mean_ps[:])
-        nc.sync.dma_start(out=out.rearrange("b (q h) -> (b q) h", h=P), in_=mean_sb[0 : B * H_BLOCKS, :])
+        first = len(COLUMN_SEQS) * H_BLOCKS
+        nc.sync.dma_start(
+            out=out[LAST : LAST + 1, :].rearrange("b (q h) -> (b q) h", h=P), in_=mean_sb[first : first + H_BLOCKS, :]
+        )
+        nc.sync.dma_start(
+            out=out[0 : len(COLUMN_SEQS), :].rearrange("b (q h) -> (b q) h", h=P), in_=mean_sb[0:first, :]
+        )

@@ -27,6 +27,9 @@ RUN = 4
 V_COLS = 592
 S_COLS = 336
 
+V_FIRST = 288
+FIRST_CUTS = (0, V_FIRST, V_COLS, H)
+
 MASKED = -1e20
 
 COLUMN_SEQS = (0, 1, 2)
@@ -66,11 +69,9 @@ def tile_selfattentionpooling_pa_t_kernel(tc, h_tanh, W2, padding_mask, data, ou
             for c in range(PASSES):
                 raw = raw_pool.tile([P, PACK, H], BF16)
                 rows = data[b, c * K_PASS : (c + 1) * K_PASS, :].rearrange("(p j) w -> p j w", j=PACK)
-                if b == 0 and c == 0:
-                    nc.sync.dma_start(out=raw[:, :, 0:V_COLS], in_=rows[:, :, 0:V_COLS])
-                    nc.sync.dma_start(out=raw[:, :, V_COLS:H], in_=rows[:, :, V_COLS:H])
-                else:
-                    nc.sync.dma_start(out=raw[:], in_=rows)
+                cuts = FIRST_CUTS if b == 0 and c == 0 else (0, H)
+                for lo, hi in zip(cuts[:-1], cuts[1:]):
+                    nc.sync.dma_start(out=raw[:, :, lo:hi], in_=rows[:, :, lo:hi])
                 raws[(b, c)] = raw
                 if c == 0 and b + 1 < B:
                     nc.sync.dma_start(out=h_sb[:, b + 1 : b + 2], in_=h_view[:, b + 1 : b + 2])
@@ -84,6 +85,8 @@ def tile_selfattentionpooling_pa_t_kernel(tc, h_tanh, W2, padding_mask, data, ou
         inv_sum = const.tile([A, B], F32)
         meanT_sb = const.tile([P, P], F32)
         nc.vector.memset(meanT_sb[:], 0.0)
+        lastT_sb = const.tile([P, P], F32)
+        nc.gpsimd.memset(lastT_sb[:], 0.0)
         meanT_ps = psum_mean.tile([P, len(COLUMN_SEQS) * H_BLOCKS], F32, tag="mean")
         one_hot = const.tile([A, len(ROW_SEQS), P], F32)
         nc.gpsimd.memset(one_hot[:], 0.0)
@@ -118,7 +121,11 @@ def tile_selfattentionpooling_pa_t_kernel(tc, h_tanh, W2, padding_mask, data, ou
 
         def scores(b):
             hT_sb = work.tile([U, S], BF16)
-            nc.scalar.copy(out=hT_sb[:], in_=hT_banks[b][:].rearrange("u g p -> u (g p)"))
+            hT_flat = hT_banks[b][:].rearrange("u g p -> u (g p)")
+            steps = PASSES if b == 0 else 1
+            for t in range(steps):
+                t_cols = slice(t * S // steps, (t + 1) * S // steps)
+                nc.scalar.copy(out=hT_sb[:, t_cols], in_=hT_flat[:, t_cols])
             for c in range(PASSES):
                 logit_ps = psum_score.tile([A, K_PASS], F32, tag="score")
                 nc.tensor.matmul(
@@ -190,13 +197,14 @@ def tile_selfattentionpooling_pa_t_kernel(tc, h_tanh, W2, padding_mask, data, ou
         def regroup_data(b, c):
             raw = raws[(b, c)]
             grouped = grouped_pool.tile([P, H, PACK], BF16, align_bytes=64)
-            v_cols = slice(0, V_COLS)
+            v_cuts = FIRST_CUTS[:-1] if b == 0 and c == 0 else (0, V_COLS)
             s_cols = slice(V_COLS, V_COLS + S_COLS)
             g_cols = slice(V_COLS + S_COLS, H)
-            nc.vector.tensor_copy(
-                out=grouped[:, v_cols, :].rearrange("p (q i) j -> p q j i", i=RUN),
-                in_=raw[:, :, v_cols].rearrange("p j (q i) -> p q j i", i=RUN),
-            )
+            for lo, hi in zip(v_cuts[:-1], v_cuts[1:]):
+                nc.vector.tensor_copy(
+                    out=grouped[:, lo:hi, :].rearrange("p (q i) j -> p q j i", i=RUN),
+                    in_=raw[:, :, lo:hi].rearrange("p j (q i) -> p q j i", i=RUN),
+                )
             nc.scalar.copy(
                 out=grouped[:, s_cols, :].rearrange("p (q i) j -> p q j i", i=RUN),
                 in_=raw[:, :, s_cols].rearrange("p j (q i) -> p q j i", i=RUN),
@@ -318,7 +326,6 @@ def tile_selfattentionpooling_pa_t_kernel(tc, h_tanh, W2, padding_mask, data, ou
                         stop=(c == PASSES - 1),
                     )
                 weighted = work.tile([P, A], F32)
-                col = len(COLUMN_SEQS) * H_BLOCKS + q
                 nc.vector.scalar_tensor_tensor(
                     out=weighted[:],
                     in0=accT_ps[:],
@@ -326,7 +333,7 @@ def tile_selfattentionpooling_pa_t_kernel(tc, h_tanh, W2, padding_mask, data, ou
                     in1=inv_row[:],
                     op0=ALU.mult,
                     op1=ALU.mult,
-                    accum_out=meanT_sb[:, col : col + 1],
+                    accum_out=lastT_sb[:, q : q + 1],
                 )
 
         transpose_hidden(0)
@@ -372,17 +379,17 @@ def tile_selfattentionpooling_pa_t_kernel(tc, h_tanh, W2, padding_mask, data, ou
                 broadcast_reciprocals(b)
             quantise_data(b, 1)
 
+        def store_columns(columns_sb, pool, tag, first_seq, seqs):
+            rows = seqs * H_BLOCKS
+            turned_ps = pool.tile([P, P], F32, tag=tag)
+            nc.tensor.transpose(turned_ps[:], columns_sb[:], ident_f32[:])
+            turned_sb = work.tile([P, P], F32)
+            nc.scalar.copy(out=turned_sb[0:rows, :], in_=turned_ps[0:rows, :])
+            nc.sync.dma_start(
+                out=out[first_seq : first_seq + seqs, :].rearrange("b (q h) -> (b q) h", h=P), in_=turned_sb[0:rows, :]
+            )
+
         attend_by_features(LAST)
         store_rows()
-
-        mean_ps = psum_score.tile([P, P], F32, tag="score")
-        nc.tensor.transpose(mean_ps[:], meanT_sb[:], ident_f32[:])
-        mean_sb = const.tile([P, P], F32)
-        nc.scalar.copy(out=mean_sb[:], in_=mean_ps[:])
-        first = len(COLUMN_SEQS) * H_BLOCKS
-        nc.sync.dma_start(
-            out=out[LAST : LAST + 1, :].rearrange("b (q h) -> (b q) h", h=P), in_=mean_sb[first : first + H_BLOCKS, :]
-        )
-        nc.sync.dma_start(
-            out=out[0 : len(COLUMN_SEQS), :].rearrange("b (q h) -> (b q) h", h=P), in_=mean_sb[0:first, :]
-        )
+        store_columns(meanT_sb, psum_acc, "acc", COLUMN_SEQS[0], len(COLUMN_SEQS))
+        store_columns(lastT_sb, psum_acc, "acc", LAST, 1)

@@ -85,8 +85,7 @@ def tile_selfattentionpooling_pa_t_kernel(tc, h_tanh, W2, padding_mask, data, ou
         inv_sum = const.tile([A, B], F32)
         meanT_sb = const.tile([P, P], F32)
         nc.vector.memset(meanT_sb[:], 0.0)
-        lastT_sb = const.tile([P, P], F32)
-        nc.gpsimd.memset(lastT_sb[:], 0.0)
+        last_sb = const.tile([P, H_BLOCKS], F32)
         meanT_ps = psum_mean.tile([P, len(COLUMN_SEQS) * H_BLOCKS], F32, tag="mean")
         one_hot = const.tile([A, len(ROW_SEQS), P], F32)
         nc.gpsimd.memset(one_hot[:], 0.0)
@@ -198,25 +197,32 @@ def tile_selfattentionpooling_pa_t_kernel(tc, h_tanh, W2, padding_mask, data, ou
             raw = raws[(b, c)]
             grouped = grouped_pool.tile([P, H, PACK], BF16, align_bytes=64)
             v_cuts = FIRST_CUTS[:-1] if b == 0 and c == 0 else (0, V_COLS)
-            s_cols = slice(V_COLS, V_COLS + S_COLS)
-            g_cols = slice(V_COLS + S_COLS, H)
-            for lo, hi in zip(v_cuts[:-1], v_cuts[1:]):
-                nc.vector.tensor_copy(
-                    out=grouped[:, lo:hi, :].rearrange("p (q i) j -> p q j i", i=RUN),
-                    in_=raw[:, :, lo:hi].rearrange("p j (q i) -> p q j i", i=RUN),
+
+            def views(lo, hi):
+                if b == LAST:
+                    halves = H_BLOCKS // RUN
+                    turned = grouped[:].rearrange("p (h i m) j -> p h m j i", h=halves, i=RUN)
+                    return (
+                        turned[:, :, lo // H_BLOCKS : hi // H_BLOCKS, :, :],
+                        raw[:, :, lo:hi].rearrange("p j (m h i) -> p h m j i", h=halves, i=RUN),
+                    )
+                return (
+                    grouped[:, lo:hi, :].rearrange("p (q i) j -> p q j i", i=RUN),
+                    raw[:, :, lo:hi].rearrange("p j (q i) -> p q j i", i=RUN),
                 )
-            nc.scalar.copy(
-                out=grouped[:, s_cols, :].rearrange("p (q i) j -> p q j i", i=RUN),
-                in_=raw[:, :, s_cols].rearrange("p j (q i) -> p q j i", i=RUN),
-            )
-            nc.gpsimd.tensor_scalar(
-                out=grouped[:, g_cols, :].rearrange("p (q i) j -> p q j i", i=RUN),
-                in0=raw[:, :, g_cols].rearrange("p j (q i) -> p q j i", i=RUN),
-                scalar1=1.0,
-                scalar2=0.0,
-                op0=ALU.mult,
-                op1=ALU.add,
-            )
+
+            for lo, hi in zip(v_cuts[:-1], v_cuts[1:]):
+                v_out, v_in = views(lo, hi)
+                nc.vector.tensor_copy(out=v_out, in_=v_in)
+            s_out, s_in = views(V_COLS, V_COLS + S_COLS)
+            nc.scalar.copy(out=s_out, in_=s_in)
+            g_out, g_in = views(V_COLS + S_COLS, H)
+            if b == LAST:
+                g_steps = [(g_out[:, h], g_in[:, h]) for h in range(H_BLOCKS // RUN)]
+            else:
+                g_steps = [(g_out, g_in)]
+            for step_out, step_in in g_steps:
+                nc.gpsimd.tensor_scalar(out=step_out, in0=step_in, scalar1=1.0, scalar2=0.0, op0=ALU.mult, op1=ALU.add)
             groupeds[(b, c)] = grouped
 
         def quantise_data(b, c):
@@ -333,7 +339,7 @@ def tile_selfattentionpooling_pa_t_kernel(tc, h_tanh, W2, padding_mask, data, ou
                     in1=inv_row[:],
                     op0=ALU.mult,
                     op1=ALU.mult,
-                    accum_out=lastT_sb[:, q : q + 1],
+                    accum_out=last_sb[:, q : q + 1],
                 )
 
         transpose_hidden(0)
@@ -392,4 +398,4 @@ def tile_selfattentionpooling_pa_t_kernel(tc, h_tanh, W2, padding_mask, data, ou
         attend_by_features(LAST)
         store_rows()
         store_columns(meanT_sb, psum_acc, "acc", COLUMN_SEQS[0], len(COLUMN_SEQS))
-        store_columns(lastT_sb, psum_acc, "acc", LAST, 1)
+        nc.sync.dma_start(out=out[LAST, :].rearrange("(m q) -> m q", q=H_BLOCKS), in_=last_sb[:])

@@ -24,7 +24,7 @@ H_BLOCKS = H // P
 PAIRS = PACK // 2
 RUN = 4
 
-V_COLS = 592
+V_COLS = 576
 S_COLS = 336
 
 V_FIRST = 288

@@ -23,6 +23,7 @@ N_TILES = H // N_TILE
 H_BLOCKS = H // P
 PAIRS = PACK // 2
 RUN = 4
+S_RUN = 8
 
 V_COLS = 576
 S_COLS = 336
@@ -198,7 +199,7 @@ def tile_selfattentionpooling_pa_t_kernel(tc, h_tanh, W2, padding_mask, data, ou
             grouped = grouped_pool.tile([P, H, PACK], BF16, align_bytes=64)
             v_cuts = FIRST_CUTS[:-1] if b == 0 and c == 0 else (0, V_COLS)
 
-            def views(lo, hi):
+            def views(lo, hi, run=RUN):
                 if b == LAST:
                     halves = H_BLOCKS // RUN
                     turned = grouped[:].rearrange("p (h i m) j -> p h m j i", h=halves, i=RUN)
@@ -207,14 +208,14 @@ def tile_selfattentionpooling_pa_t_kernel(tc, h_tanh, W2, padding_mask, data, ou
                         raw[:, :, lo:hi].rearrange("p j (m h i) -> p h m j i", h=halves, i=RUN),
                     )
                 return (
-                    grouped[:, lo:hi, :].rearrange("p (q i) j -> p q j i", i=RUN),
-                    raw[:, :, lo:hi].rearrange("p j (q i) -> p q j i", i=RUN),
+                    grouped[:, lo:hi, :].rearrange("p (q i) j -> p q j i", i=run),
+                    raw[:, :, lo:hi].rearrange("p j (q i) -> p q j i", i=run),
                 )
 
             for lo, hi in zip(v_cuts[:-1], v_cuts[1:]):
                 v_out, v_in = views(lo, hi)
                 nc.vector.tensor_copy(out=v_out, in_=v_in)
-            s_out, s_in = views(V_COLS, V_COLS + S_COLS)
+            s_out, s_in = views(V_COLS, V_COLS + S_COLS, S_RUN)
             nc.scalar.copy(out=s_out, in_=s_in)
             g_out, g_in = views(V_COLS + S_COLS, H)
             if b == LAST:

from contextlib import ExitStack

import concourse.mybir as mybir
from concourse.masks import make_identity

BF16 = mybir.dt.bfloat16
F32 = mybir.dt.float32
U32 = mybir.dt.uint32
U8 = mybir.dt.uint8
FP8X4 = mybir.dt.float8_e4m3fn_x4
ALU = mybir.AluOpType
ACT = mybir.ActivationFunctionType
AXIS = mybir.AxisListType

B, S, H, U, A = 8, 1024, 1024, 128, 128
P = 128
PACK = 4
K_PASS = P * PACK
PASSES = S // K_PASS
GROUPS = PASSES * PACK
N_TILE = 512
N_TILES = H // N_TILE
H_BLOCKS = H // P
PAIRS = PACK // 2
RUN = 4
S_RUN = 8

V_COLS = 576
S_COLS = 336

V_FIRST = 288
FIRST_CUTS = (0, V_FIRST, V_COLS, H)

MASKED = -1e20

COLUMN_SEQS = (0, 1, 2)
ROW_SEQS = (3, 4, 5, 6)
LAST = 7

FLOPS = 2 * B * S * U * A + 2 * B * A * S * H


def tile_selfattentionpooling_pa_t_kernel(tc, h_tanh, W2, padding_mask, data, out):
    nc = tc.nc
    with ExitStack() as ctx:
        const = ctx.enter_context(tc.tile_pool(name="const", bufs=1))
        raw_pool = ctx.enter_context(tc.tile_pool(name="raw", bufs=8))
        grouped_pool = ctx.enter_context(tc.tile_pool(name="grouped", bufs=3))
        codes_pool = ctx.enter_context(tc.tile_pool(name="codes", bufs=2 * PASSES))
        work = ctx.enter_context(tc.tile_pool(name="work", bufs=2))
        psum_t = ctx.enter_context(tc.psum_pool(name="psum_t", bufs=2))
        psum_score = ctx.enter_context(tc.psum_pool(name="psum_score", bufs=2))
        psum_acc = ctx.enter_context(tc.psum_pool(name="psum_acc", bufs=N_TILES))
        psum_mean = ctx.enter_context(tc.psum_pool(name="psum_mean", bufs=2))
        ctx.enter_context(tc.manual_schedule())

        mask_rows = const.tile([P, K_PASS], BF16)
        nc.vector.memset(mask_rows[:], 0.0)
        w2_sb = const.tile([U, A], BF16)
        nc.sync.dma_start(out=w2_sb[:], in_=W2[:, :])
        h_sb = const.tile([P, B, PASSES, PACK * U], BF16)
        h_view = h_tanh.rearrange("b (c p j) u -> p b c (j u)", c=PASSES, p=P, j=PACK)
        nc.sync.dma_start(out=h_sb[:, 0:1], in_=h_view[:, 0:1])
        nc.sync.dma_start(
            out=mask_rows[0 : B * PASSES, :], in_=padding_mask.rearrange("b (c k) -> (b c) k", k=K_PASS)
        )

        raws = {}
        for b in range(B):
            for c in range(PASSES):
                raw = raw_pool.tile([P, PACK, H], BF16)
                rows = data[b, c * K_PASS : (c + 1) * K_PASS, :].rearrange("(p j) w -> p j w", j=PACK)
                cuts = FIRST_CUTS if b == 0 and c == 0 else (0, H)
                for lo, hi in zip(cuts[:-1], cuts[1:]):
                    nc.sync.dma_start(out=raw[:, :, lo:hi], in_=rows[:, :, lo:hi])
                raws[(b, c)] = raw
                if c == 0 and b + 1 < B:
                    nc.sync.dma_start(out=h_sb[:, b + 1 : b + 2], in_=h_view[:, b + 1 : b + 2])

        ident_bf = const.tile([P, P], BF16)
        make_identity(nc, ident_bf[:])
        ident_f32 = const.tile([P, P], F32)
        make_identity(nc, ident_f32[:])
        bank_sum = const.tile([A, B, PASSES], F32)
        colsum = const.tile([A, B], F32)
        inv_sum = const.tile([A, B], F32)
        meanT_sb = const.tile([P, P], F32)
        nc.vector.memset(meanT_sb[:], 0.0)
        last_sb = const.tile([P, H_BLOCKS], F32)
        meanT_ps = psum_mean.tile([P, len(COLUMN_SEQS) * H_BLOCKS], F32, tag="mean")
        one_hot = const.tile([A, len(ROW_SEQS), P], F32)
        nc.gpsimd.memset(one_hot[:], 0.0)
        inv_row = const.tile([P, A], F32)
        rows_sb = const.tile([P, H], F32)
        row_banks = []

        maskT_ps = psum_t.tile([P, PACK, P], BF16, tag="t16")
        for j in range(PACK):
            nc.tensor.transpose(
                maskT_ps[:, j, :], mask_rows[:].rearrange("r (p j) -> r j p", j=PACK)[:, j, :], ident_bf[:]
            )
        penalty = const.tile([P, PACK, B * PASSES], F32)
        nc.vector.tensor_scalar(
            out=penalty[:],
            in0=maskT_ps[:, :, 0 : B * PASSES],
            scalar1=1.0,
            scalar2=-MASKED,
            op0=ALU.subtract,
            op1=ALU.mult,
        )

        hT_banks, score_banks, bank_maxes, neg_maxes, eT_banks = {}, {}, {}, {}, {}
        e_groupeds, e_words, d_words, groupeds, acc_banks, attendeds = {}, {}, {}, {}, {}, {}

        def transpose_hidden(b):
            hT_ps = psum_t.tile([U, GROUPS, P], BF16, tag="t16")
            for c in range(PASSES):
                for j in range(PACK):
                    nc.tensor.transpose(hT_ps[:, c * PACK + j, :], h_sb[:, b, c, j * U : (j + 1) * U], ident_bf[:])
            hT_banks[b] = hT_ps

        def scores(b):
            hT_sb = work.tile([U, S], BF16)
            hT_flat = hT_banks[b][:].rearrange("u g p -> u (g p)")
            steps = PASSES if b == 0 else 1
            for t in range(steps):
                t_cols = slice(t * S // steps, (t + 1) * S // steps)
                nc.scalar.copy(out=hT_sb[:, t_cols], in_=hT_flat[:, t_cols])
            for c in range(PASSES):
                logit_ps = psum_score.tile([A, K_PASS], F32, tag="score")
                nc.tensor.matmul(
                    logit_ps[:], lhsT=w2_sb[:], rhs=hT_sb[:, c * K_PASS : (c + 1) * K_PASS], start=True, stop=False
                )
                row = b * PASSES + c
                for j in range(PACK):
                    nc.tensor.matmul(
                        logit_ps[:, j * P : (j + 1) * P],
                        lhsT=penalty[:, j, row : row + 1].to_broadcast([P, A]),
                        rhs=ident_f32[:],
                        is_transpose=True,
                        start=False,
                        stop=(j == PACK - 1),
                    )
                score_banks[(b, c)] = logit_ps

        def bank_maxima(b):
            bank_max = work.tile([A, PASSES], F32)
            for c in range(PASSES):
                nc.vector.tensor_reduce(out=bank_max[:, c : c + 1], in_=score_banks[(b, c)][:], axis=AXIS.X, op=ALU.max)
            bank_maxes[b] = bank_max

        def negative_maximum(b):
            neg_max = work.tile([A, 1], F32)
            nc.vector.tensor_reduce(out=neg_max[:], in_=bank_maxes[b][:], axis=AXIS.X, op=ALU.max, negate=True)
            neg_maxes[b] = neg_max

        def exponentials(b):
            e_sb = work.tile([A, S], BF16)
            for c in range(PASSES):
                nc.scalar.activation(
                    out=e_sb[:, c * K_PASS : (c + 1) * K_PASS].rearrange("a (p j) -> a p j", j=PACK),
                    in_=score_banks[(b, c)][:].rearrange("a (j p) -> a p j", j=PACK),
                    func=ACT.Exp,
                    bias=neg_maxes[b][:],
                    scale=1.0,
                    accum_out=bank_sum[:, b, c : c + 1],
                )
            e_pairs = e_sb[:].bitcast(F32)
            eT_ps = psum_t.tile([P, PASSES, PAIRS, A], F32, tag="t16")
            for c in range(PASSES):
                for u in range(PAIRS):
                    nc.tensor.transpose(
                        eT_ps[:, c, u, :],
                        e_pairs[:, c * PAIRS * P + u : (c + 1) * PAIRS * P : PAIRS],
                        ident_f32[:],
                    )
            eT_banks[b] = eT_ps

        def regroup_e(b):
            e_grouped = work.tile([P, PASSES * A * PACK], BF16, align_bytes=64)
            nc.scalar.copy(
                out=e_grouped[:].bitcast(F32).rearrange("p (c a u) -> p c a u", c=PASSES, u=PAIRS),
                in_=eT_banks[b][:].rearrange("p c u a -> p c a u"),
            )
            e_groupeds[b] = e_grouped

        def quantise_e(b):
            e_codes = work.tile([P, PASSES * A], U32, align_bytes=64)
            e_scales = work.tile([P, PASSES * A], U8, align_bytes=64)
            nc.vector.quantize_mx(
                out=e_codes[:].bitcast(FP8X4),
                scales=e_scales[:],
                in_=e_groupeds[b][:],
            )
            e_words[b] = (e_codes, e_scales)

        def regroup_data(b, c):
            raw = raws[(b, c)]
            grouped = grouped_pool.tile([P, H, PACK], BF16, align_bytes=64)
            v_cuts = FIRST_CUTS[:-1] if b == 0 and c == 0 else (0, V_COLS)

            def views(lo, hi, run=RUN):
                if b == LAST:
                    halves = H_BLOCKS // RUN
                    turned = grouped[:].rearrange("p (h i m) j -> p h m j i", h=halves, i=RUN)
                    return (
                        turned[:, :, lo // H_BLOCKS : hi // H_BLOCKS, :, :],
                        raw[:, :, lo:hi].rearrange("p j (m h i) -> p h m j i", h=halves, i=RUN),
                    )
                return (
                    grouped[:, lo:hi, :].rearrange("p (q i) j -> p q j i", i=run),
                    raw[:, :, lo:hi].rearrange("p j (q i) -> p q j i", i=run),
                )

            for lo, hi in zip(v_cuts[:-1], v_cuts[1:]):
                v_out, v_in = views(lo, hi)
                nc.vector.tensor_copy(out=v_out, in_=v_in)
            s_out, s_in = views(V_COLS, V_COLS + S_COLS, S_RUN)
            nc.scalar.copy(out=s_out, in_=s_in)
            g_out, g_in = views(V_COLS + S_COLS, H)
            if b == LAST:
                g_steps = [(g_out[:, h], g_in[:, h]) for h in range(H_BLOCKS // RUN)]
            else:
                g_steps = [(g_out, g_in)]
            for step_out, step_in in g_steps:
                nc.gpsimd.tensor_scalar(out=step_out, in0=step_in, scalar1=1.0, scalar2=0.0, op0=ALU.mult, op1=ALU.add)
            groupeds[(b, c)] = grouped

        def quantise_data(b, c):
            d_codes = codes_pool.tile([P, H], U32, align_bytes=64)
            d_scales = codes_pool.tile([P, H], U8, align_bytes=64)
            nc.vector.quantize_mx(
                out=d_codes[:].bitcast(FP8X4),
                scales=d_scales[:],
                in_=groupeds[(b, c)][:].rearrange("p w j -> p (w j)"),
            )
            d_words[(b, c)] = (d_codes, d_scales)

        def attend(b):
            e_codes, e_scales = e_words[b]
            banks = []
            for n in range(N_TILES):
                acc_ps = psum_acc.tile([A, N_TILE], F32, tag="acc")
                n_cols = slice(n * N_TILE, (n + 1) * N_TILE)
                for c in range(PASSES):
                    d_codes, d_scales = d_words[(b, c)]
                    a_cols = slice(c * A, (c + 1) * A)
                    nc.tensor.matmul_mx(
                        out=acc_ps[:],
                        lhsT=e_codes[:, a_cols].bitcast(FP8X4),
                        lhsT_scale=e_scales[:, a_cols],
                        rhs=d_codes[:, n_cols].bitcast(FP8X4),
                        rhs_scale=d_scales[:, n_cols],
                        start=(c == 0),
                        stop=(c == PASSES - 1),
                    )
                banks.append(acc_ps)
            acc_banks[b] = banks

        def sum_e(b):
            nc.vector.tensor_reduce(out=colsum[:, b : b + 1], in_=bank_sum[:, b, :], axis=AXIS.X, op=ALU.add)

        def reciprocal_sum(b):
            if b in ROW_SEQS:
                r = ROW_SEQS.index(b)
                nc.vector.reciprocal(out=one_hot[:, r, r : r + 1], in_=colsum[:, b : b + 1])
            else:
                nc.vector.reciprocal(out=inv_sum[:, b : b + 1], in_=colsum[:, b : b + 1])

        def copy_attended(b, n):
            if n == 0:
                acc_sb = work.tile([A, H], F32)
                attendeds[b] = acc_sb
            nc.scalar.copy(out=attendeds[b][:, n * N_TILE : (n + 1) * N_TILE], in_=acc_banks[b][n][:])

        def mean_over_heads(b):
            for q in range(H_BLOCKS):
                col = b * H_BLOCKS + q
                nc.tensor.matmul(
                    meanT_ps[:, col : col + 1],
                    lhsT=attendeds[b][:, q * P : (q + 1) * P],
                    rhs=inv_sum[:, b : b + 1],
                    start=True,
                    stop=True,
                )

        def mean_as_row(b):
            r = ROW_SEQS.index(b)
            for n in range(N_TILES):
                if r == 0:
                    row_ps = psum_mean.tile([P, N_TILE], F32, tag="mean")
                    row_banks.append(row_ps)
                nc.tensor.matmul(
                    row_banks[n][:],
                    lhsT=one_hot[:, r, :],
                    rhs=attendeds[b][:, n * N_TILE : (n + 1) * N_TILE],
                    start=(r == 0),
                    stop=(r == len(ROW_SEQS) - 1),
                )

        def copy_columns():
            cols = len(COLUMN_SEQS) * H_BLOCKS
            nc.scalar.mul(out=meanT_sb[:, 0:cols], in_=meanT_ps[:], mul=1.0 / A)

        def store_rows():
            rows = len(ROW_SEQS)
            for n in range(N_TILES):
                nc.scalar.mul(out=rows_sb[0:rows, n * N_TILE : (n + 1) * N_TILE], in_=row_banks[n][0:rows, :], mul=1.0 / A)
            nc.sync.dma_start(out=out[ROW_SEQS[0] : ROW_SEQS[0] + rows, :], in_=rows_sb[0:rows, :])

        def broadcast_reciprocals(b):
            bc_ps = psum_t.tile([P, A], F32, tag="t16")
            nc.tensor.transpose(bc_ps[:], inv_sum[:, b : b + 1].to_broadcast([A, P]), ident_f32[:])
            nc.scalar.mul(out=inv_row[:], in_=bc_ps[:], mul=1.0 / A)

        def attend_by_features(b):
            e_codes, e_scales = e_words[b]
            spare = [(psum_score, "score"), (psum_score, "score"), (psum_acc, "acc"), (psum_acc, "acc"), (psum_t, "t16"), (psum_t, "t16")]
            for q in range(H_BLOCKS):
                pool, tag = spare[q % len(spare)]
                accT_ps = pool.tile([P, A], F32, tag=tag)
                w_cols = slice(q * P, (q + 1) * P)
                for c in range(PASSES):
                    d_codes, d_scales = d_words[(b, c)]
                    a_cols = slice(c * A, (c + 1) * A)
                    nc.tensor.matmul_mx(
                        out=accT_ps[:],
                        lhsT=d_codes[:, w_cols].bitcast(FP8X4),
                        lhsT_scale=d_scales[:, w_cols],
                        rhs=e_codes[:, a_cols].bitcast(FP8X4),
                        rhs_scale=e_scales[:, a_cols],
                        start=(c == 0),
                        stop=(c == PASSES - 1),
                    )
                weighted = work.tile([P, A], F32)
                nc.vector.scalar_tensor_tensor(
                    out=weighted[:],
                    in0=accT_ps[:],
                    scalar=1.0,
                    in1=inv_row[:],
                    op0=ALU.mult,
                    op1=ALU.mult,
                    accum_out=last_sb[:, q : q + 1],
                )

        transpose_hidden(0)
        scores(0)
        for b in range(B):
            has_last = b >= 1
            has_next = b + 1 < B
            regroup_data(b, 0)
            bank_maxima(b)
            if has_last:
                quantise_e(b - 1)
            negative_maximum(b)
            if has_last:
                sum_e(b - 1)
                attend(b - 1)
            if has_next:
                transpose_hidden(b + 1)
            regroup_data(b, 1)
            if has_last:
                reciprocal_sum(b - 1)
            exponentials(b)
            if has_last:
                copy_attended(b - 1, 0)
            if not has_next:
                regroup_e(b)
            if has_last:
                copy_attended(b - 1, 1)
            if b - 1 == ROW_SEQS[0]:
                copy_columns()
            if has_next:
                scores(b + 1)
            if b - 1 in COLUMN_SEQS:
                mean_over_heads(b - 1)
            if b - 1 in ROW_SEQS:
                mean_as_row(b - 1)
            quantise_data(b, 0)
            if has_next:
                regroup_e(b)
            else:
                sum_e(b)
                quantise_e(b)
                reciprocal_sum(b)
                broadcast_reciprocals(b)
            quantise_data(b, 1)

        def store_columns(columns_sb, pool, tag, first_seq, seqs):
            rows = seqs * H_BLOCKS
            turned_ps = pool.tile([P, P], F32, tag=tag)
            nc.tensor.transpose(turned_ps[:], columns_sb[:], ident_f32[:])
            turned_sb = work.tile([P, P], F32)
            nc.scalar.copy(out=turned_sb[0:rows, :], in_=turned_ps[0:rows, :])
            nc.sync.dma_start(
                out=out[first_seq : first_seq + seqs, :].rearrange("b (q h) -> (b q) h", h=P), in_=turned_sb[0:rows, :]
            )

        attend_by_features(LAST)
        store_rows()
        store_columns(meanT_sb, psum_acc, "acc", COLUMN_SEQS[0], len(COLUMN_SEQS))
        nc.sync.dma_start(out=out[LAST, :].rearrange("(m q) -> m q", q=H_BLOCKS), in_=last_sb[:])
